import numpy as np
import ml_dtypes

BF16 = ml_dtypes.bfloat16


def bf(x):
    return np.asarray(x, np.float32).astype(BF16)


def f32(x):
    return np.asarray(x, np.float32)


def f64(x):
    return np.asarray(x).astype(np.float64)


def striped(idx):
    return np.tile(idx.reshape(-1, 16).T, (8, 1))


C, S, N, Q, K, H, D, R = 1024, 1024, 16384, 128, 128, 8, 8192, 512


def setup_inputs():
    idx = np.concatenate([np.random.permutation(S)[:R] for _ in range(N // R)])
    return {"qh": bf(np.random.standard_normal((H, D, Q))), "kh": bf(np.random.standard_normal((H, D, K))), "w": f32(3.0 * np.random.standard_normal((C, S))), "offs": striped(idx)}


def reference(qh, kh, w, offs):
    idx = offs[:16].T.reshape(-1)
    score = np.matmul(f64(qh).transpose(0, 2, 1), f64(kh)) / np.sqrt(D)
    e = np.exp(score - score.max(axis=-1, keepdims=True))
    p = e / e.sum(axis=-1, keepdims=True)
    attn = p.sum(axis=0) / H
    picked = f64(w)[:, idx].reshape(C, Q, K)
    return np.einsum('cat,at->ca', picked, attn)

@@ -1,0 +1,120 @@
+import math
+
+import concourse.mybir as mybir
+from concourse.masks import make_identity
+
+BF16, F32, U16 = mybir.dt.bfloat16, mybir.dt.float32, mybir.dt.uint16
+MULT, ADD = mybir.AluOpType.mult, mybir.AluOpType.add
+EXP, COPY = mybir.ActivationFunctionType.Exp, mybir.ActivationFunctionType.Copy
+
+P = 128
+H, D, Q, K = 8, 8192, 128, 128
+C, S = 1024, 1024
+N = Q * K
+FLOPS = 2 * H * D * Q * K + 2 * C * N
+
+D_TILES = D // P
+CHUNK = 32
+C_BLOCKS = C // P
+PIECE = 1024
+Q_PIECE = PIECE // K
+PIECES = N // PIECE
+BANK = 512
+Q_BANK = BANK // K
+
+
+def tile_evl_b_kernel(tc, qh, kh, w, offs, out):
+    nc = tc.nc
+    with (
+        tc.tile_pool(name="held", bufs=1) as held,
+        tc.tile_pool(name="stats", bufs=2) as stats,
+        tc.psum_pool(name="score_psum", bufs=2) as score_psum,
+        tc.psum_pool(name="spread_psum", bufs=4) as spread_psum,
+    ):
+        offsets = held.tile([P, N // 16], U16, name="offsets")
+        nc.sync.dma_start(offsets[:], offs)
+
+        ident = held.tile([P, P], BF16, name="ident")
+        make_identity(nc, ident[:])
+        pick = held.tile([P, Q, P], BF16, name="pick")
+        nc.vector.tensor_copy(pick[:], ident[:].unsqueeze(2).to_broadcast([P, Q, P]))
+
+        attn_sum = held.tile([P, K], F32, name="attn_sum")
+        attn_bf = held.tile([P, K], BF16, name="attn_bf")
+        with tc.tile_pool(name="qk", bufs=6) as qk:
+            for h in range(H):
+                q_rows = qh[h].rearrange("(p j) a -> p j a", p=P)
+                k_rows = kh[h].rearrange("(p j) t -> p j t", p=P)
+                score = score_psum.tile([P, K], F32, name="score")
+                for j0 in range(0, D_TILES, CHUNK):
+                    q_sb = qk.tile([P, CHUNK, Q], BF16, name="q_sb")
+                    k_sb = qk.tile([P, CHUNK, K], BF16, name="k_sb")
+                    nc.sync.dma_start(q_sb[:], q_rows[:, j0 : j0 + CHUNK, :])
+                    nc.scalar.dma_start(k_sb[:], k_rows[:, j0 : j0 + CHUNK, :])
+                    for j in range(CHUNK):
+                        nc.tensor.matmul(
+                            score[:], q_sb[:, j, :], k_sb[:, j, :],
+                            start=(j0 + j == 0), stop=(j0 + j == D_TILES - 1),
+                        )
+                scale = 1.0 / math.sqrt(D)
+                top = stats.tile([P, 1], F32, name="top")
+                nc.vector.reduce_max(top[:], score[:], axis=mybir.AxisListType.X)
+                shift = stats.tile([P, 1], F32, name="shift")
+                nc.vector.tensor_scalar_mul(shift[:], top[:], -scale)
+                e = stats.tile([P, K], F32, name="e")
+                total = stats.tile([P, 1], F32, name="total")
+                nc.scalar.activation(e[:], score[:], EXP, bias=shift[:], scale=scale, accum_out=total[:])
+                inv = stats.tile([P, 1], F32, name="inv")
+                nc.vector.reciprocal(inv[:], total[:])
+                if h == 0:
+                    nc.vector.tensor_scalar_mul(attn_sum[:], e[:], inv[:])
+                else:
+                    target = attn_bf if h == H - 1 else attn_sum
+                    nc.vector.scalar_tensor_tensor(target[:], e[:], inv[:], attn_sum[:], MULT, ADD)
+
+        with (
+            tc.tile_pool(name="table", bufs=1) as table,
+            tc.tile_pool(name="spread", bufs=2) as spread,
+            tc.tile_pool(name="products", bufs=4) as products,
+        ):
+            w_sb = []
+            out_sb = []
+            for b in range(C_BLOCKS):
+                w_sb.append(table.tile([P, S], F32, name="w_sb%d" % b))
+                nc.sync.dma_start(w_sb[b][:], w[b * P : (b + 1) * P, :])
+                out_sb.append(table.tile([P, Q], F32, name="out_sb%d" % b))
+
+            def spread_piece(piece):
+                attn_row = spread.tile([P, PIECE], F32, name="attn_row")
+                for bank in range(PIECE // BANK):
+                    spread_ps = spread_psum.tile([P, BANK], F32, name="spread_ps")
+                    for i in range(Q_BANK):
+                        a = piece * Q_PIECE + bank * Q_BANK + i
+                        nc.tensor.matmul(
+                            spread_ps[:, i * K : (i + 1) * K], pick[:, a, :], attn_bf[:],
+                            start=True, stop=True,
+                        )
+                    nc.scalar.activation(
+                        attn_row[:, bank * BANK : (bank + 1) * BANK], spread_ps[:], COPY, scale=1.0 / H
+                    )
+                return attn_row
+
+            attn_next = spread_piece(0)
+            for piece in range(PIECES):
+                attn_row = attn_next
+                if piece + 1 < PIECES:
+                    attn_next = spread_piece(piece + 1)
+                piece_offsets = offsets[:, piece * (PIECE // 16) : (piece + 1) * (PIECE // 16)]
+                for b in range(C_BLOCKS):
+                    product = products.tile([P, PIECE], F32, name="product")
+                    nc.vector.tensor_tensor(
+                        product[:], w_sb[b][:].indirect(piece_offsets), attn_row[:], MULT
+                    )
+                    for i in range(Q_PIECE):
+                        a = piece * Q_PIECE + i
+                        nc.scalar.activation(
+                            product[:, i * K : (i + 1) * K], product[:, i * K : (i + 1) * K], COPY,
+                            accum_out=out_sb[b][:, a : a + 1],
+                        )
+            for b in range(C_BLOCKS):
+                nc.sync.dma_start(out[b * P : (b + 1) * P, :], out_sb[b][:])

@@ -14,7 +14,7 @@ N = Q * K
 FLOPS = 2 * H * D * Q * K + 2 * C * N
 
 D_TILES = D // P
-CHUNK = 32
+LAST_HEAD_LOADS = 4
 C_BLOCKS = C // P
 PIECE = 1024
 Q_PIECE = PIECE // K
@@ -41,21 +41,22 @@ def tile_evl_b_kernel(tc, qh, kh, w, offs, out):
 
         attn_sum = held.tile([P, K], F32, name="attn_sum")
         attn_bf = held.tile([P, K], BF16, name="attn_bf")
-        with tc.tile_pool(name="qk", bufs=6) as qk:
+        with tc.tile_pool(name="qk", bufs=3) as qk:
             for h in range(H):
                 q_rows = qh[h].rearrange("(p j) a -> p j a", p=P)
                 k_rows = kh[h].rearrange("(p j) t -> p j t", p=P)
+                q_sb = qk.tile([P, D_TILES, Q], BF16, name="q_sb")
+                k_sb = qk.tile([P, D_TILES, K], BF16, name="k_sb")
+                step = D_TILES // (LAST_HEAD_LOADS if h == H - 1 else 1)
+                for j0 in range(0, D_TILES, step):
+                    nc.sync.dma_start(q_sb[:, j0 : j0 + step, :], q_rows[:, j0 : j0 + step, :])
+                    nc.scalar.dma_start(k_sb[:, j0 : j0 + step, :], k_rows[:, j0 : j0 + step, :])
                 score = score_psum.tile([P, K], F32, name="score")
-                for j0 in range(0, D_TILES, CHUNK):
-                    q_sb = qk.tile([P, CHUNK, Q], BF16, name="q_sb")
-                    k_sb = qk.tile([P, CHUNK, K], BF16, name="k_sb")
-                    nc.sync.dma_start(q_sb[:], q_rows[:, j0 : j0 + CHUNK, :])
-                    nc.scalar.dma_start(k_sb[:], k_rows[:, j0 : j0 + CHUNK, :])
-                    for j in range(CHUNK):
-                        nc.tensor.matmul(
-                            score[:], q_sb[:, j, :], k_sb[:, j, :],
-                            start=(j0 + j == 0), stop=(j0 + j == D_TILES - 1),
-                        )
+                for j in range(D_TILES):
+                    nc.tensor.matmul(
+                        score[:], q_sb[:, j, :], k_sb[:, j, :],
+                        start=(j == 0), stop=(j == D_TILES - 1),
+                    )
                 scale = 1.0 / math.sqrt(D)
                 top = stats.tile([P, 1], F32, name="top")
                 nc.vector.reduce_max(top[:], score[:], axis=mybir.AxisListType.X)

@@ -21,6 +21,8 @@ Q_PIECE = PIECE // K
 PIECES = N // PIECE
 BANK = 512
 Q_BANK = BANK // K
+FIRST_CUT = [Q_BANK, Q_PIECE - Q_BANK]
+LAST_CUT = [Q_PIECE // 2, 2, 2]
 
 
 def tile_evl_b_kernel(tc, qh, kh, w, offs, out):
@@ -41,7 +43,7 @@ def tile_evl_b_kernel(tc, qh, kh, w, offs, out):
 
         attn_sum = held.tile([P, K], F32, name="attn_sum")
         attn_bf = held.tile([P, K], BF16, name="attn_bf")
-        with tc.tile_pool(name="qk", bufs=3) as qk:
+        with tc.tile_pool(name="qk", bufs=4) as qk:
             for h in range(H):
                 q_rows = qh[h].rearrange("(p j) a -> p j a", p=P)
                 k_rows = kh[h].rearrange("(p j) t -> p j t", p=P)
@@ -74,7 +76,7 @@ def tile_evl_b_kernel(tc, qh, kh, w, offs, out):
                     nc.vector.scalar_tensor_tensor(target[:], e[:], inv[:], attn_sum[:], MULT, ADD)
 
         with (
-            tc.tile_pool(name="table", bufs=1) as table,
+            tc.tile_pool(name="table", bufs=1, reuse_waits="tile") as table,
             tc.tile_pool(name="spread", bufs=2) as spread,
             tc.tile_pool(name="products", bufs=4) as products,
         ):
@@ -105,17 +107,27 @@ def tile_evl_b_kernel(tc, qh, kh, w, offs, out):
                 attn_row = attn_next
                 if piece + 1 < PIECES:
                     attn_next = spread_piece(piece + 1)
-                piece_offsets = offsets[:, piece * (PIECE // 16) : (piece + 1) * (PIECE // 16)]
                 for b in range(C_BLOCKS):
-                    product = products.tile([P, PIECE], F32, name="product")
-                    nc.vector.tensor_tensor(
-                        product[:], w_sb[b][:].indirect(piece_offsets), attn_row[:], MULT
-                    )
-                    for i in range(Q_PIECE):
-                        a = piece * Q_PIECE + i
-                        nc.scalar.activation(
-                            product[:, i * K : (i + 1) * K], product[:, i * K : (i + 1) * K], COPY,
-                            accum_out=out_sb[b][:, a : a + 1],
+                    if piece == 0 and b == 0:
+                        cut = FIRST_CUT
+                    elif piece == PIECES - 1 and b == C_BLOCKS - 1:
+                        cut = LAST_CUT
+                    else:
+                        cut = [Q_PIECE]
+                    for part, queries in enumerate(cut):
+                        i0 = sum(cut[:part])
+                        a0 = piece * Q_PIECE + i0
+                        product = products.tile([P, PIECE], F32, name="product")
+                        nc.vector.tensor_tensor(
+                            product[:, : queries * K],
+                            w_sb[b][:].indirect(offsets[:, a0 * K // 16 : (a0 + queries) * K // 16]),
+                            attn_row[:, i0 * K : (i0 + queries) * K],
+                            MULT,
                         )
+                        for i in range(queries):
+                            nc.scalar.activation(
+                                product[:, i * K : (i + 1) * K], product[:, i * K : (i + 1) * K], COPY,
+                                accum_out=out_sb[b][:, a0 + i : a0 + i + 1],
+                            )
             for b in range(C_BLOCKS):
                 nc.sync.dma_start(out[b * P : (b + 1) * P, :], out_sb[b][:])

@@ -14,7 +14,7 @@ N = Q * K
 FLOPS = 2 * H * D * Q * K + 2 * C * N
 
 D_TILES = D // P
-LAST_HEAD_LOADS = 4
+LAST_LOAD = 8
 C_BLOCKS = C // P
 PIECE = 1024
 Q_PIECE = PIECE // K
@@ -49,10 +49,13 @@ def tile_evl_b_kernel(tc, qh, kh, w, offs, out):
                 k_rows = kh[h].rearrange("(p j) t -> p j t", p=P)
                 q_sb = qk.tile([P, D_TILES, Q], BF16, name="q_sb")
                 k_sb = qk.tile([P, D_TILES, K], BF16, name="k_sb")
-                step = D_TILES // (LAST_HEAD_LOADS if h == H - 1 else 1)
-                for j0 in range(0, D_TILES, step):
+                j0 = 0
+                while j0 < D_TILES:
+                    left = D_TILES - j0
+                    step = left // 2 if h == H - 1 and left > LAST_LOAD else left
                     nc.sync.dma_start(q_sb[:, j0 : j0 + step, :], q_rows[:, j0 : j0 + step, :])
                     nc.scalar.dma_start(k_sb[:, j0 : j0 + step, :], k_rows[:, j0 : j0 + step, :])
+                    j0 += step
                 score = score_psum.tile([P, K], F32, name="score")
                 for j in range(D_TILES):
                     nc.tensor.matmul(

@@ -4,7 +4,7 @@ import concourse.mybir as mybir
 from concourse.masks import make_identity
 
 BF16, F32, U16 = mybir.dt.bfloat16, mybir.dt.float32, mybir.dt.uint16
-MULT, ADD = mybir.AluOpType.mult, mybir.AluOpType.add
+MULT, ADD, MIN = mybir.AluOpType.mult, mybir.AluOpType.add, mybir.AluOpType.min
 EXP, COPY = mybir.ActivationFunctionType.Exp, mybir.ActivationFunctionType.Copy
 
 P = 128
@@ -21,7 +21,8 @@ Q_PIECE = PIECE // K
 PIECES = N // PIECE
 BANK = 512
 Q_BANK = BANK // K
-FIRST_CUT = [Q_BANK, Q_PIECE - Q_BANK]
+FIRST_CUT = [2, 2, Q_PIECE - 4]
+assert max(FIRST_CUT) <= Q_BANK and sum(FIRST_CUT) == Q_PIECE
 LAST_CUT = [Q_PIECE // 2, 2, 2]
 
 
@@ -63,10 +64,9 @@ def tile_evl_b_kernel(tc, qh, kh, w, offs, out):
                         start=(j == 0), stop=(j == D_TILES - 1),
                     )
                 scale = 1.0 / math.sqrt(D)
-                top = stats.tile([P, 1], F32, name="top")
-                nc.vector.reduce_max(top[:], score[:], axis=mybir.AxisListType.X)
+                negated = stats.tile([P, K], F32, name="negated")
                 shift = stats.tile([P, 1], F32, name="shift")
-                nc.vector.tensor_scalar_mul(shift[:], top[:], -scale)
+                nc.vector.tensor_scalar(negated[:], score[:], -scale, None, MULT, MIN, accum_out=shift[:])
                 e = stats.tile([P, K], F32, name="e")
                 total = stats.tile([P, 1], F32, name="total")
                 nc.scalar.activation(e[:], score[:], EXP, bias=shift[:], scale=scale, accum_out=total[:])
@@ -92,16 +92,18 @@ def tile_evl_b_kernel(tc, qh, kh, w, offs, out):
 
             def spread_piece(piece):
                 attn_row = spread.tile([P, PIECE], F32, name="attn_row")
-                for bank in range(PIECE // BANK):
+                groups = FIRST_CUT if piece == 0 else [Q_BANK] * (Q_PIECE // Q_BANK)
+                for group, queries in enumerate(groups):
+                    i0 = sum(groups[:group])
                     spread_ps = spread_psum.tile([P, BANK], F32, name="spread_ps")
-                    for i in range(Q_BANK):
-                        a = piece * Q_PIECE + bank * Q_BANK + i
+                    for i in range(queries):
                         nc.tensor.matmul(
-                            spread_ps[:, i * K : (i + 1) * K], pick[:, a, :], attn_bf[:],
-                            start=True, stop=True,
+                            spread_ps[:, i * K : (i + 1) * K], pick[:, piece * Q_PIECE + i0 + i, :],
+                            attn_bf[:], start=True, stop=True,
                         )
                     nc.scalar.activation(
-                        attn_row[:, bank * BANK : (bank + 1) * BANK], spread_ps[:], COPY, scale=1.0 / H
+                        attn_row[:, i0 * K : (i0 + queries) * K], spread_ps[:, : queries * K], COPY,
+                        scale=1.0 / H,
                     )
                 return attn_row
 

@@ -44,6 +44,11 @@ def tile_evl_b_kernel(tc, qh, kh, w, offs, out):
 
         attn_sum = held.tile([P, K], F32, name="attn_sum")
         attn_bf = held.tile([P, K], BF16, name="attn_bf")
+        inv_row = held.tile([P, Q], F32, name="inv_row")
+        ident_f32 = held.tile([P, P], F32, name="ident_f32")
+        make_identity(nc, ident_f32[:])
+        ones_f32 = held.tile([P, P], F32, name="ones_f32")
+        nc.vector.memset(ones_f32[:], 1.0)
         with tc.tile_pool(name="qk", bufs=4) as qk:
             for h in range(H):
                 q_rows = qh[h].rearrange("(p j) a -> p j a", p=P)
@@ -71,12 +76,19 @@ def tile_evl_b_kernel(tc, qh, kh, w, offs, out):
                 total = stats.tile([P, 1], F32, name="total")
                 nc.scalar.activation(e[:], score[:], EXP, bias=shift[:], scale=scale, accum_out=total[:])
                 inv = stats.tile([P, 1], F32, name="inv")
+                if h == H - 1:
+                    nc.vector.scalar_tensor_tensor(attn_bf[:], attn_sum[:], total[:], e[:], MULT, ADD)
                 nc.vector.reciprocal(inv[:], total[:])
                 if h == 0:
                     nc.vector.tensor_scalar_mul(attn_sum[:], e[:], inv[:])
+                elif h < H - 1:
+                    nc.vector.scalar_tensor_tensor(attn_sum[:], e[:], inv[:], attn_sum[:], MULT, ADD)
                 else:
-                    target = attn_bf if h == H - 1 else attn_sum
-                    nc.vector.scalar_tensor_tensor(target[:], e[:], inv[:], attn_sum[:], MULT, ADD)
+                    diag = stats.tile([P, Q], F32, name="diag")
+                    nc.vector.tensor_scalar(diag[:], ident_f32[:], inv[:], 1.0 / H, MULT, MULT)
+                    inv_ps = score_psum.tile([P, Q], F32, name="score")
+                    nc.tensor.matmul(inv_ps[:], ones_f32[:], diag[:], start=True, stop=True)
+                    nc.scalar.copy(inv_row[:], inv_ps[:])
 
         with (
             tc.tile_pool(name="table", bufs=1, reuse_waits="tile") as table,
@@ -101,10 +113,8 @@ def tile_evl_b_kernel(tc, qh, kh, w, offs, out):
                             spread_ps[:, i * K : (i + 1) * K], pick[:, piece * Q_PIECE + i0 + i, :],
                             attn_bf[:], start=True, stop=True,
                         )
-                    nc.scalar.activation(
-                        attn_row[:, i0 * K : (i0 + queries) * K], spread_ps[:, : queries * K], COPY,
-                        scale=1.0 / H,
-                    )
+                    copier = nc.vector.tensor_copy if piece == 0 and group == 0 else nc.scalar.copy
+                    copier(attn_row[:, i0 * K : (i0 + queries) * K], spread_ps[:, : queries * K])
                 return attn_row
 
             attn_next = spread_piece(0)
@@ -132,6 +142,7 @@ def tile_evl_b_kernel(tc, qh, kh, w, offs, out):
                         for i in range(queries):
                             nc.scalar.activation(
                                 product[:, i * K : (i + 1) * K], product[:, i * K : (i + 1) * K], COPY,
+                                scale=inv_row[:, a0 + i : a0 + i + 1],
                                 accum_out=out_sb[b][:, a0 + i : a0 + i + 1],
                             )
             for b in range(C_BLOCKS):

@@ -35,7 +35,6 @@ def tile_evl_b_kernel(tc, qh, kh, w, offs, out):
         tc.psum_pool(name="spread_psum", bufs=4) as spread_psum,
     ):
         offsets = held.tile([P, N // 16], U16, name="offsets")
-        nc.sync.dma_start(offsets[:], offs)
 
         ident = held.tile([P, P], BF16, name="ident")
         make_identity(nc, ident[:])
@@ -49,12 +48,12 @@ def tile_evl_b_kernel(tc, qh, kh, w, offs, out):
         make_identity(nc, ident_f32[:])
         ones_f32 = held.tile([P, P], F32, name="ones_f32")
         nc.vector.memset(ones_f32[:], 1.0)
-        with tc.tile_pool(name="qk", bufs=4) as qk:
+        with tc.tile_pool(name="q_pool", bufs=H) as q_pool, tc.tile_pool(name="k_pool", bufs=4) as k_pool:
             for h in range(H):
                 q_rows = qh[h].rearrange("(p j) a -> p j a", p=P)
                 k_rows = kh[h].rearrange("(p j) t -> p j t", p=P)
-                q_sb = qk.tile([P, D_TILES, Q], BF16, name="q_sb")
-                k_sb = qk.tile([P, D_TILES, K], BF16, name="k_sb")
+                q_sb = q_pool.tile([P, D_TILES, Q], BF16, name="q_sb")
+                k_sb = k_pool.tile([P, D_TILES, K], BF16, name="k_sb")
                 j0 = 0
                 while j0 < D_TILES:
                     left = D_TILES - j0
@@ -89,6 +88,7 @@ def tile_evl_b_kernel(tc, qh, kh, w, offs, out):
                     inv_ps = score_psum.tile([P, Q], F32, name="score")
                     nc.tensor.matmul(inv_ps[:], ones_f32[:], diag[:], start=True, stop=True)
                     nc.scalar.copy(inv_row[:], inv_ps[:])
+            nc.sync.dma_start(offsets[:], offs)
 
         with (
             tc.tile_pool(name="table", bufs=1, reuse_waits="tile") as table,

@@ -48,18 +48,27 @@ def tile_evl_b_kernel(tc, qh, kh, w, offs, out):
         make_identity(nc, ident_f32[:])
         ones_f32 = held.tile([P, P], F32, name="ones_f32")
         nc.vector.memset(ones_f32[:], 1.0)
-        with tc.tile_pool(name="q_pool", bufs=H) as q_pool, tc.tile_pool(name="k_pool", bufs=4) as k_pool:
+        with (
+            tc.tile_pool(name="q_pool", bufs=H) as q_pool,
+            tc.tile_pool(name="k_pool", bufs=3) as k_pool,
+            tc.tile_pool(name="k_last_pool", bufs=1) as k_last_pool,
+        ):
             for h in range(H):
                 q_rows = qh[h].rearrange("(p j) a -> p j a", p=P)
                 k_rows = kh[h].rearrange("(p j) t -> p j t", p=P)
                 q_sb = q_pool.tile([P, D_TILES, Q], BF16, name="q_sb")
-                k_sb = k_pool.tile([P, D_TILES, K], BF16, name="k_sb")
+                if h == H - 1:
+                    k_sb = k_last_pool.tile([P, D_TILES, K], BF16, name="k_sb")
+                    k_queue = nc.sync
+                else:
+                    k_sb = k_pool.tile([P, D_TILES, K], BF16, name="k_sb")
+                    k_queue = nc.scalar
                 j0 = 0
                 while j0 < D_TILES:
                     left = D_TILES - j0
                     step = left // 2 if h == H - 1 and left > LAST_LOAD else left
                     nc.sync.dma_start(q_sb[:, j0 : j0 + step, :], q_rows[:, j0 : j0 + step, :])
-                    nc.scalar.dma_start(k_sb[:, j0 : j0 + step, :], k_rows[:, j0 : j0 + step, :])
+                    k_queue.dma_start(k_sb[:, j0 : j0 + step, :], k_rows[:, j0 : j0 + step, :])
                     j0 += step
                 score = score_psum.tile([P, K], F32, name="score")
                 for j in range(D_TILES):

import math

import concourse.mybir as mybir
from concourse.masks import make_identity

BF16, F32, U16 = mybir.dt.bfloat16, mybir.dt.float32, mybir.dt.uint16
MULT, ADD, MIN = mybir.AluOpType.mult, mybir.AluOpType.add, mybir.AluOpType.min
EXP, COPY = mybir.ActivationFunctionType.Exp, mybir.ActivationFunctionType.Copy

P = 128
H, D, Q, K = 8, 8192, 128, 128
C, S = 1024, 1024
N = Q * K
FLOPS = 2 * H * D * Q * K + 2 * C * N

D_TILES = D // P
LAST_LOAD = 8
C_BLOCKS = C // P
PIECE = 1024
Q_PIECE = PIECE // K
PIECES = N // PIECE
BANK = 512
Q_BANK = BANK // K
FIRST_CUT = [2, 2, Q_PIECE - 4]
assert max(FIRST_CUT) <= Q_BANK and sum(FIRST_CUT) == Q_PIECE
LAST_CUT = [Q_PIECE // 2, 2, 2]


def tile_evl_b_kernel(tc, qh, kh, w, offs, out):
    nc = tc.nc
    with (
        tc.tile_pool(name="held", bufs=1) as held,
        tc.tile_pool(name="stats", bufs=2) as stats,
        tc.psum_pool(name="score_psum", bufs=2) as score_psum,
        tc.psum_pool(name="spread_psum", bufs=4) as spread_psum,
    ):
        offsets = held.tile([P, N // 16], U16, name="offsets")

        ident = held.tile([P, P], BF16, name="ident")
        make_identity(nc, ident[:])
        pick = held.tile([P, Q, P], BF16, name="pick")
        nc.vector.tensor_copy(pick[:], ident[:].unsqueeze(2).to_broadcast([P, Q, P]))

        attn_sum = held.tile([P, K], F32, name="attn_sum")
        attn_bf = held.tile([P, K], BF16, name="attn_bf")
        inv_row = held.tile([P, Q], F32, name="inv_row")
        ident_f32 = held.tile([P, P], F32, name="ident_f32")
        make_identity(nc, ident_f32[:])
        ones_f32 = held.tile([P, P], F32, name="ones_f32")
        nc.vector.memset(ones_f32[:], 1.0)
        with (
            tc.tile_pool(name="q_pool", bufs=H) as q_pool,
            tc.tile_pool(name="k_pool", bufs=3) as k_pool,
            tc.tile_pool(name="k_last_pool", bufs=1) as k_last_pool,
        ):
            for h in range(H):
                q_rows = qh[h].rearrange("(p j) a -> p j a", p=P)
                k_rows = kh[h].rearrange("(p j) t -> p j t", p=P)
                q_sb = q_pool.tile([P, D_TILES, Q], BF16, name="q_sb")
                if h == H - 1:
                    k_sb = k_last_pool.tile([P, D_TILES, K], BF16, name="k_sb")
                    k_queue = nc.sync
                else:
                    k_sb = k_pool.tile([P, D_TILES, K], BF16, name="k_sb")
                    k_queue = nc.scalar
                j0 = 0
                while j0 < D_TILES:
                    left = D_TILES - j0
                    step = left // 2 if h == H - 1 and left > LAST_LOAD else left
                    nc.sync.dma_start(q_sb[:, j0 : j0 + step, :], q_rows[:, j0 : j0 + step, :])
                    k_queue.dma_start(k_sb[:, j0 : j0 + step, :], k_rows[:, j0 : j0 + step, :])
                    j0 += step
                score = score_psum.tile([P, K], F32, name="score")
                for j in range(D_TILES):
                    nc.tensor.matmul(
                        score[:], q_sb[:, j, :], k_sb[:, j, :],
                        start=(j == 0), stop=(j == D_TILES - 1),
                    )
                scale = 1.0 / math.sqrt(D)
                negated = stats.tile([P, K], F32, name="negated")
                shift = stats.tile([P, 1], F32, name="shift")
                nc.vector.tensor_scalar(negated[:], score[:], -scale, None, MULT, MIN, accum_out=shift[:])
                e = stats.tile([P, K], F32, name="e")
                total = stats.tile([P, 1], F32, name="total")
                nc.scalar.activation(e[:], score[:], EXP, bias=shift[:], scale=scale, accum_out=total[:])
                inv = stats.tile([P, 1], F32, name="inv")
                if h == H - 1:
                    nc.vector.scalar_tensor_tensor(attn_bf[:], attn_sum[:], total[:], e[:], MULT, ADD)
                nc.vector.reciprocal(inv[:], total[:])
                if h == 0:
                    nc.vector.tensor_scalar_mul(attn_sum[:], e[:], inv[:])
                elif h < H - 1:
                    nc.vector.scalar_tensor_tensor(attn_sum[:], e[:], inv[:], attn_sum[:], MULT, ADD)
                else:
                    diag = stats.tile([P, Q], F32, name="diag")
                    nc.vector.tensor_scalar(diag[:], ident_f32[:], inv[:], 1.0 / H, MULT, MULT)
                    inv_ps = score_psum.tile([P, Q], F32, name="score")
                    nc.tensor.matmul(inv_ps[:], ones_f32[:], diag[:], start=True, stop=True)
                    nc.scalar.copy(inv_row[:], inv_ps[:])
            nc.sync.dma_start(offsets[:], offs)

        with (
            tc.tile_pool(name="table", bufs=1, reuse_waits="tile") as table,
            tc.tile_pool(name="spread", bufs=2) as spread,
            tc.tile_pool(name="products", bufs=4) as products,
        ):
            w_sb = []
            out_sb = []
            for b in range(C_BLOCKS):
                w_sb.append(table.tile([P, S], F32, name="w_sb%d" % b))
                nc.sync.dma_start(w_sb[b][:], w[b * P : (b + 1) * P, :])
                out_sb.append(table.tile([P, Q], F32, name="out_sb%d" % b))

            def spread_piece(piece):
                attn_row = spread.tile([P, PIECE], F32, name="attn_row")
                groups = FIRST_CUT if piece == 0 else [Q_BANK] * (Q_PIECE // Q_BANK)
                for group, queries in enumerate(groups):
                    i0 = sum(groups[:group])
                    spread_ps = spread_psum.tile([P, BANK], F32, name="spread_ps")
                    for i in range(queries):
                        nc.tensor.matmul(
                            spread_ps[:, i * K : (i + 1) * K], pick[:, piece * Q_PIECE + i0 + i, :],
                            attn_bf[:], start=True, stop=True,
                        )
                    copier = nc.vector.tensor_copy if piece == 0 and group == 0 else nc.scalar.copy
                    copier(attn_row[:, i0 * K : (i0 + queries) * K], spread_ps[:, : queries * K])
                return attn_row

            attn_next = spread_piece(0)
            for piece in range(PIECES):
                attn_row = attn_next
                if piece + 1 < PIECES:
                    attn_next = spread_piece(piece + 1)
                for b in range(C_BLOCKS):
                    if piece == 0 and b == 0:
                        cut = FIRST_CUT
                    elif piece == PIECES - 1 and b == C_BLOCKS - 1:
                        cut = LAST_CUT
                    else:
                        cut = [Q_PIECE]
                    for part, queries in enumerate(cut):
                        i0 = sum(cut[:part])
                        a0 = piece * Q_PIECE + i0
                        product = products.tile([P, PIECE], F32, name="product")
                        nc.vector.tensor_tensor(
                            product[:, : queries * K],
                            w_sb[b][:].indirect(offsets[:, a0 * K // 16 : (a0 + queries) * K // 16]),
                            attn_row[:, i0 * K : (i0 + queries) * K],
                            MULT,
                        )
                        for i in range(queries):
                            nc.scalar.activation(
                                product[:, i * K : (i + 1) * K], product[:, i * K : (i + 1) * K], COPY,
                                scale=inv_row[:, a0 + i : a0 + i + 1],
                                accum_out=out_sb[b][:, a0 + i : a0 + i + 1],
                            )
            for b in range(C_BLOCKS):
                nc.sync.dma_start(out[b * P : (b + 1) * P, :], out_sb[b][:])
